import numpy as np
import ml_dtypes


BF16 = ml_dtypes.bfloat16


def bf(x):
    return np.asarray(x, np.float32).astype(BF16)


def f64(x):
    return np.asarray(x).astype(np.float64)


E2M1 = np.array([0.0, 0.5, 1.0, 1.5, 2.0, 3.0, 4.0, 6.0, -0.0, -0.5, -1.0, -1.5, -2.0, -3.0, -4.0, -6.0])


def pack_weight(w, fmt):
    k, n = w.shape
    w = f64(bf(w)).reshape(k // 32, 32, n)
    amax = np.abs(w).max(1)
    if fmt == "e4m3":
        byte = np.frexp(amax)[1] - 1 + 127 - 7
    else:
        mant, ex = np.frexp(amax / 6.0)
        byte = np.where(mant > 0.5, ex, ex - 1) + 127
    byte = np.clip(np.where(amax > 0, byte, 1), 1, 254)
    scaled = (w * np.exp2(127.0 - byte)[:, None, :]).reshape(k, n).astype(np.float32)
    by_word = np.ascontiguousarray(scaled.reshape(k // 512, 128, 4, n).transpose(0, 1, 3, 2))
    if fmt == "e4m3":
        words = by_word.astype(ml_dtypes.float8_e4m3fn).view(np.uint8)
    else:
        c = by_word.astype(ml_dtypes.float4_e2m1fn).view(np.uint8) & 0xF
        words = c[..., 0::2] | (c[..., 1::2] << 4)
    return np.ascontiguousarray(words), np.ascontiguousarray(byte.astype(np.uint8).reshape(k // 512, 16, n))


def unpack_weight(words, scales, fmt):
    g, p, n, _ = words.shape
    if fmt == "e4m3":
        vals = np.ascontiguousarray(words).view(ml_dtypes.float8_e4m3fn).astype(np.float64)
    else:
        nib = np.empty((g, p, n, 4), np.uint8)
        nib[..., 0::2] = words & 0xF
        nib[..., 1::2] = words >> 4
        vals = E2M1[nib]
    vals = vals * np.repeat(np.exp2(scales.astype(np.float64) - 127.0), 8, axis=1)[..., None]
    return vals.transpose(0, 1, 3, 2).reshape(g * 512, n)

def pack4(w):
    words, scales = pack_weight(w, "e2m1")
    return words.reshape(words.shape[0], 128, -1), scales


def unpack4(words, scales):
    return unpack_weight(words.reshape(words.shape[0], 128, -1, 2), scales, "e2m1")


def kspread(k):
    return np.exp2(np.repeat(np.random.randint(-6, 7, k // 32), 32).astype(np.float64))


B, S, HID, NH, NKV, HD, QB = 2, 512, 2048, 8, 2, 128, 512
THETA = 10000.0
SCALING = 1.0
HALF = HD // 2
NQ = NH * HD
NK = NKV * HD


def rope_tables(n):
    inv_freq = 1.0 / THETA ** (np.arange(0, HD, 2) / HD)
    t = np.arange(n) / SCALING
    freqs = t[:, None] * inv_freq[None, :]
    emb = np.concatenate([freqs, freqs], axis=-1)
    return np.cos(emb), np.sin(emb)


def rotate_half(x):
    return np.concatenate([-x[..., HALF:], x[..., :HALF]], axis=-1)


def apply_rope(x, cos, sin):
    return x * cos[None, None] + rotate_half(x) * sin[None, None]


def setup_inputs():
    s = kspread(HID)
    hidden_states = np.random.standard_normal((B, S, HID)) * s
    hidden_states_words, hidden_states_scales = pack4(hidden_states.reshape(B * S, HID).T)
    words, scales = pack4(np.random.standard_normal((HID, NQ + 2 * NK)) / np.sqrt(HID) / s[:, None])
    return {"hidden_states_words": hidden_states_words,
            "hidden_states_scales": hidden_states_scales,
            "W_qkv_words": words,
            "W_qkv_scales": scales}


def reference(hidden_states_words, hidden_states_scales, W_qkv_words, W_qkv_scales):
    h = unpack4(hidden_states_words, hidden_states_scales).T.reshape(B, S, HID)
    qkv = h @ unpack4(W_qkv_words, W_qkv_scales)
    q = qkv[..., :NQ].reshape(B, S, NH, HD).transpose(0, 2, 1, 3)
    k = qkv[..., NQ:NQ + NK].reshape(B, S, NKV, HD).transpose(0, 2, 1, 3)
    v = qkv[..., NQ + NK:].reshape(B, S, NKV, HD).transpose(0, 2, 1, 3)
    cos, sin = rope_tables(S)
    return apply_rope(q, cos, sin), apply_rope(k, cos, sin), v

@@ -1,0 +1,225 @@
+from contextlib import ExitStack
+
+import concourse.mybir as mybir
+
+BATCH, SEQ, HID = 2, 512, 2048
+NH, NKV, HD = 8, 2, 128
+HALF = HD // 2
+P = 128
+K_PASS = 512
+PASSES = HID // K_PASS
+N_TILE = 512
+POS_TILES = SEQ // P
+FLOPS = 2 * BATCH * SEQ * HID * (NH + 2 * NKV) * HD
+
+F32 = mybir.dt.float32
+BF16 = mybir.dt.bfloat16
+I32 = mybir.dt.int32
+U8 = mybir.dt.uint8
+FP4X4 = mybir.dt.float4_e2m1fn_x4
+ALU = mybir.AluOpType
+ACT = mybir.ActivationFunctionType
+
+TWO_PI = 6.283185307179586
+WARM_UP = 8
+
+
+def split_turns(d):
+    g = 10000.0 ** (-d / 64.0) / TWO_PI
+    k = 0
+    while g * 2.0 ** k < 16384.0:
+        k += 1
+    hi = int(g * 2.0 ** k) / 2.0 ** k
+    return hi, g - hi
+
+
+def tile_fastmultiheadattention_pa_kernel(
+    tc, hidden_states_words, hidden_states_scales, W_qkv_words, W_qkv_scales, out_0, out_1, out_2
+):
+    nc = tc.nc
+    with ExitStack() as ctx:
+        keep = ctx.enter_context(tc.tile_pool(name="keep", bufs=1))
+        work = ctx.enter_context(tc.tile_pool(name="work", bufs=6))
+        psum = ctx.enter_context(tc.psum_pool(name="psum", bufs=8))
+
+        def load_codes(words, c, name, queue, view):
+            codes = keep.tile([P, PASSES, 2 * N_TILE], U8, name=name, align_bytes=64)
+            queue.dma_start(
+                out=codes[:].bitcast(view),
+                in_=words[:, :, 2 * N_TILE * c : 2 * N_TILE * (c + 1)].rearrange("g p n -> p g n").bitcast(view),
+            )
+            return codes
+
+        def zero_planes(name):
+            planes = keep.tile([P, PASSES, N_TILE], U8, name=name, align_bytes=64)
+            nc.vector.memset(planes[:].bitcast(I32), 0)
+            return planes
+
+        def load_planes(planes, scales, c):
+            for q in range(4):
+                nc.sync.dma_start(
+                    out=planes[32 * q : 32 * q + 4, :, :].bitcast(I32),
+                    in_=scales[:, 4 * q : 4 * q + 4, N_TILE * c : N_TILE * (c + 1)]
+                    .rearrange("g r n -> r g n")
+                    .bitcast(I32),
+                )
+
+        zero = keep.tile([P, 1], F32, name="zero")
+        nc.vector.memset(zero[:], 0.0)
+        warm = keep.tile([P, 1], F32, name="warm")
+        nc.scalar.activation(out=warm[:], in_=zero[:], func=ACT.Sin)
+        pos = keep.tile([P, POS_TILES], F32, name="pos")
+        nc.gpsimd.iota(
+            pos[:], pattern=[[P, POS_TILES]], base=0, channel_multiplier=1, allow_small_or_imprecise_dtypes=True
+        )
+
+        h_planes = {0: zero_planes("h_planes0")}
+        w_planes = {0: zero_planes("w_planes0")}
+        load_planes(h_planes[0], hidden_states_scales, 0)
+        h_codes = {0: load_codes(hidden_states_words, 0, "h_codes0", nc.sync, I32)}
+        w_codes = {0: load_codes(W_qkv_words, 0, "w_codes0", nc.sync, I32)}
+        load_planes(w_planes[0], W_qkv_scales, 0)
+
+        if WARM_UP:
+            idle_in = keep.tile([P, N_TILE], BF16, name="idle_in")
+            nc.vector.memset(idle_in[:], 0.0)
+            idle_out = psum.tile([P, N_TILE], F32, name="acc")
+            for r in range(WARM_UP):
+                nc.tensor.matmul(out=idle_out[:], lhsT=idle_in[:, :P], rhs=idle_in[:], start=True, stop=True)
+
+        for n in (1, 2):
+            w_planes[n] = zero_planes("w_planes%d" % n)
+            w_codes[n] = load_codes(W_qkv_words, n, "w_codes%d" % n, nc.sync, I32)
+            load_planes(w_planes[n], W_qkv_scales, n)
+        h_planes[1] = zero_planes("h_planes1")
+        h_codes[1] = load_codes(hidden_states_words, 1, "h_codes1", nc.sync, I32)
+        load_planes(h_planes[1], hidden_states_scales, 1)
+
+        step = keep.tile([P, 2], F32, name="step")
+        nc.gpsimd.iota(step[:], pattern=[[1, 2]], base=0, channel_multiplier=0, allow_small_or_imprecise_dtypes=True)
+        per_turn = keep.tile([P, 2, HALF], F32, name="per_turn")
+        turns_hi = keep.tile([P, POS_TILES, HALF], F32, name="turns_hi")
+        turns_lo = keep.tile([P, POS_TILES, HALF], F32, name="turns_lo")
+        for part, dst, v_from in ((0, turns_hi, 40), (1, turns_lo, 40)):
+            for d in range(0, HALF, 2):
+                first, second = split_turns(d)[part], split_turns(d + 1)[part]
+                if d < v_from:
+                    nc.scalar.activation(
+                        out=per_turn[:, part, d : d + 2], in_=step[:], func=ACT.Copy, scale=second - first, bias=first
+                    )
+                else:
+                    nc.vector.tensor_scalar(
+                        out=per_turn[:, part, d : d + 2],
+                        in0=step[:],
+                        scalar1=second - first,
+                        scalar2=first,
+                        op0=ALU.mult,
+                        op1=ALU.add,
+                    )
+            nc.vector.tensor_tensor(
+                out=dst[:],
+                in0=per_turn[:, part : part + 1, :].to_broadcast([P, POS_TILES, HALF]),
+                in1=pos[:].unsqueeze(2).to_broadcast([P, POS_TILES, HALF]),
+                op=ALU.mult,
+            )
+        whole_i = keep.tile([P, POS_TILES, HALF], I32, name="whole_i")
+        nc.vector.tensor_copy(out=whole_i[:], in_=turns_hi[:])
+        frac = keep.tile([P, POS_TILES, HALF], F32, name="frac")
+        nc.vector.tensor_tensor(out=frac[:], in0=turns_hi[:], in1=whole_i[:], op=ALU.subtract)
+        turn = keep.tile([P, POS_TILES, HALF], F32, name="turn")
+        nc.vector.tensor_tensor(out=turn[:], in0=frac[:], in1=turns_lo[:], op=ALU.add)
+        minus_c = keep.tile([P, POS_TILES, HALF], F32, name="minus_c")
+        nc.vector.scalar_tensor_tensor(
+            out=minus_c[:], in0=turn[:], scalar=0.25, in1=turn[:], op0=ALU.is_gt, op1=ALU.subtract
+        )
+        minus_s = keep.tile([P, POS_TILES, HALF], F32, name="minus_s")
+        nc.vector.scalar_tensor_tensor(
+            out=minus_s[:], in0=turn[:], scalar=0.5, in1=turn[:], op0=ALU.is_gt, op1=ALU.subtract
+        )
+        cos = keep.tile([P, POS_TILES, HALF], F32, name="cos")
+        sin = keep.tile([P, POS_TILES, HALF], F32, name="sin")
+        nsin = keep.tile([P, POS_TILES, HALF], F32, name="nsin")
+        nc.scalar.activation(out=cos[:], in_=minus_c[:], func=ACT.Sin, scale=-TWO_PI, bias=TWO_PI / 4.0)
+        nc.scalar.activation(out=nsin[:], in_=minus_s[:], func=ACT.Sin, scale=TWO_PI)
+        nc.scalar.activation(out=sin[:], in_=minus_s[:], func=ACT.Sin, scale=-TWO_PI)
+
+        def project(m, c0, width):
+            b, i = divmod(m, POS_TILES)
+            n, c = divmod(c0, N_TILE)
+            acc = psum.tile([P, width], F32, name="acc")
+            for g in range(PASSES):
+                nc.tensor.matmul_mx(
+                    out=acc[:],
+                    lhsT=h_codes[b][:, g, 2 * P * i : 2 * P * (i + 1)].bitcast(FP4X4),
+                    lhsT_scale=h_planes[b][:, g, P * i : P * (i + 1)],
+                    rhs=w_codes[n][:, g, 2 * c : 2 * (c + width)].bitcast(FP4X4),
+                    rhs_scale=w_planes[n][:, g, c : c + width],
+                    start=(g == 0),
+                    stop=(g == PASSES - 1),
+                )
+            return acc
+
+        def rope(acc, heads, i, dst, add_engine):
+            width = heads * HD
+            halves = acc.rearrange("p (h t d) -> p h t d", t=2, d=HALF)
+            straight = work.tile([P, N_TILE], F32, name="straight")
+            nc.vector.tensor_tensor(
+                out=straight[:, :width].rearrange("p (a d) -> p a d", d=HALF),
+                in0=acc.rearrange("p (a d) -> p a d", d=HALF),
+                in1=cos[:, i : i + 1, :].to_broadcast([P, 2 * heads, HALF]),
+                op=ALU.mult,
+            )
+            crossed = work.tile([P, N_TILE], F32, name="crossed")
+            crossed_halves = crossed[:, :width].rearrange("p (h t d) -> p h t d", t=2, d=HALF)
+            nc.vector.tensor_tensor(
+                out=crossed_halves[:, :, 0, :],
+                in0=halves[:, :, 1, :],
+                in1=nsin[:, i : i + 1, :].to_broadcast([P, heads, HALF]),
+                op=ALU.mult,
+            )
+            nc.vector.tensor_tensor(
+                out=crossed_halves[:, :, 1, :],
+                in0=halves[:, :, 0, :],
+                in1=sin[:, i : i + 1, :].to_broadcast([P, heads, HALF]),
+                op=ALU.mult,
+            )
+            rotated = work.tile([P, N_TILE], F32, name="rotated")
+            add_engine.tensor_tensor(
+                out=rotated[:, :width], in0=straight[:, :width], in1=crossed[:, :width], op=ALU.add
+            )
+            nc.sync.dma_start(
+                out=dst.rearrange("h p d -> p h d"),
+                in_=rotated[:, :width].rearrange("p (h d) -> p h d", d=HD),
+            )
+
+        def queries(m, n, add_engine):
+            b, i = divmod(m, POS_TILES)
+            acc = project(m, N_TILE * n, N_TILE)
+            rope(acc[:], 4, i, out_0[b, 4 * n : 4 * n + 4, P * i : P * (i + 1), :], add_engine)
+
+        def keys(m, add_engine):
+            b, i = divmod(m, POS_TILES)
+            acc = project(m, NH * HD, NKV * HD)
+            rope(acc[:], NKV, i, out_1[b, :, P * i : P * (i + 1), :], add_engine)
+
+        def values(m):
+            b, i = divmod(m, POS_TILES)
+            acc = project(m, (NH + NKV) * HD, NKV * HD)
+            plain = keep.tile([P, NKV * HD], F32, name="plain%d" % m)
+            nc.scalar.copy(out=plain[:], in_=acc[:])
+            nc.scalar.dma_start(
+                out=out_2[b, :, P * i : P * (i + 1), :].rearrange("h p d -> p h d"),
+                in_=plain[:].rearrange("p (h d) -> p h d", d=HD),
+            )
+
+        for m in range(4):
+            queries(m, 0, nc.gpsimd)
+        for m in range(4):
+            queries(m, 1, nc.gpsimd)
+            keys(m, nc.vector)
+        for m in range(4, 8):
+            queries(m, 0, nc.gpsimd)
+            queries(m, 1, nc.gpsimd)
+            keys(m, nc.vector)
+        for m in range(8):
+            values(m)

@@ -39,7 +39,7 @@ def tile_fastmultiheadattention_pa_kernel(
     nc = tc.nc
     with ExitStack() as ctx:
         keep = ctx.enter_context(tc.tile_pool(name="keep", bufs=1))
-        work = ctx.enter_context(tc.tile_pool(name="work", bufs=6))
+        work = ctx.enter_context(tc.tile_pool(name="work", bufs=4))
         psum = ctx.enter_context(tc.psum_pool(name="psum", bufs=8))
 
         def load_codes(words, c, name, queue, view):
@@ -87,7 +87,7 @@ def tile_fastmultiheadattention_pa_kernel(
             for r in range(WARM_UP):
                 nc.tensor.matmul(out=idle_out[:], lhsT=idle_in[:, :P], rhs=idle_in[:], start=True, stop=True)
 
-        for n in (1, 2):
+        for n in (2, 1):
             w_planes[n] = zero_planes("w_planes%d" % n)
             w_codes[n] = load_codes(W_qkv_words, n, "w_codes%d" % n, nc.sync, I32)
             load_planes(w_planes[n], W_qkv_scales, n)
@@ -137,11 +137,10 @@ def tile_fastmultiheadattention_pa_kernel(
             out=minus_s[:], in0=turn[:], scalar=0.5, in1=turn[:], op0=ALU.is_gt, op1=ALU.subtract
         )
         cos = keep.tile([P, POS_TILES, HALF], F32, name="cos")
-        sin = keep.tile([P, POS_TILES, HALF], F32, name="sin")
-        nsin = keep.tile([P, POS_TILES, HALF], F32, name="nsin")
+        cross = keep.tile([P, POS_TILES, 2, HALF], F32, name="cross")
         nc.scalar.activation(out=cos[:], in_=minus_c[:], func=ACT.Sin, scale=-TWO_PI, bias=TWO_PI / 4.0)
-        nc.scalar.activation(out=nsin[:], in_=minus_s[:], func=ACT.Sin, scale=TWO_PI)
-        nc.scalar.activation(out=sin[:], in_=minus_s[:], func=ACT.Sin, scale=-TWO_PI)
+        nc.scalar.activation(out=cross[:, :, 0, :], in_=minus_s[:], func=ACT.Sin, scale=TWO_PI)
+        nc.scalar.activation(out=cross[:, :, 1, :], in_=minus_s[:], func=ACT.Sin, scale=-TWO_PI)
 
         def project(m, c0, width):
             b, i = divmod(m, POS_TILES)
@@ -159,48 +158,43 @@ def tile_fastmultiheadattention_pa_kernel(
                 )
             return acc
 
-        def rope(acc, heads, i, dst, add_engine):
-            width = heads * HD
-            halves = acc.rearrange("p (h t d) -> p h t d", t=2, d=HALF)
-            straight = work.tile([P, N_TILE], F32, name="straight")
-            nc.vector.tensor_tensor(
-                out=straight[:, :width].rearrange("p (a d) -> p a d", d=HALF),
-                in0=acc.rearrange("p (a d) -> p a d", d=HALF),
-                in1=cos[:, i : i + 1, :].to_broadcast([P, 2 * heads, HALF]),
-                op=ALU.mult,
-            )
-            crossed = work.tile([P, N_TILE], F32, name="crossed")
-            crossed_halves = crossed[:, :width].rearrange("p (h t d) -> p h t d", t=2, d=HALF)
-            nc.vector.tensor_tensor(
-                out=crossed_halves[:, :, 0, :],
-                in0=halves[:, :, 1, :],
-                in1=nsin[:, i : i + 1, :].to_broadcast([P, heads, HALF]),
-                op=ALU.mult,
-            )
-            nc.vector.tensor_tensor(
-                out=crossed_halves[:, :, 1, :],
-                in0=halves[:, :, 0, :],
-                in1=sin[:, i : i + 1, :].to_broadcast([P, heads, HALF]),
-                op=ALU.mult,
-            )
-            rotated = work.tile([P, N_TILE], F32, name="rotated")
+        def rope_pair(groups, add_engine):
+            width = groups[0][2] * HD
+            straight = work.tile([P, 2 * N_TILE], F32, name="straight")
+            crossed = work.tile([P, 2 * N_TILE], F32, name="crossed")
+            rotated = work.tile([P, 2 * N_TILE], F32, name="rotated")
+            for j, (m, c0, heads, dst) in enumerate(groups):
+                i = m % POS_TILES
+                cols = slice(j * width, (j + 1) * width)
+                acc = project(m, c0, width)
+                nc.vector.tensor_tensor(
+                    out=straight[:, cols].rearrange("p (a d) -> p a d", d=HALF),
+                    in0=acc[:].rearrange("p (a d) -> p a d", d=HALF),
+                    in1=cos[:, i : i + 1, :].to_broadcast([P, 2 * heads, HALF]),
+                    op=ALU.mult,
+                )
+                nc.vector.tensor_tensor(
+                    out=crossed[:, cols].rearrange("p (h t d) -> p h t d", t=2, d=HALF),
+                    in0=acc[:].rearrange("p (h t d) -> p h t d", t=2, d=HALF)[:, :, ::-1, :],
+                    in1=cross[:, i : i + 1, :, :].to_broadcast([P, heads, 2, HALF]),
+                    op=ALU.mult,
+                )
             add_engine.tensor_tensor(
-                out=rotated[:, :width], in0=straight[:, :width], in1=crossed[:, :width], op=ALU.add
+                out=rotated[:, : 2 * width], in0=straight[:, : 2 * width], in1=crossed[:, : 2 * width], op=ALU.add
             )
-            nc.sync.dma_start(
-                out=dst.rearrange("h p d -> p h d"),
-                in_=rotated[:, :width].rearrange("p (h d) -> p h d", d=HD),
-            )
+            for j, (m, c0, heads, dst) in enumerate(groups):
+                nc.sync.dma_start(
+                    out=dst.rearrange("h p d -> p h d"),
+                    in_=rotated[:, j * width : (j + 1) * width].rearrange("p (h d) -> p h d", d=HD),
+                )
 
-        def queries(m, n, add_engine):
+        def query_group(m, n):
             b, i = divmod(m, POS_TILES)
-            acc = project(m, N_TILE * n, N_TILE)
-            rope(acc[:], 4, i, out_0[b, 4 * n : 4 * n + 4, P * i : P * (i + 1), :], add_engine)
+            return (m, N_TILE * n, 4, out_0[b, 4 * n : 4 * n + 4, P * i : P * (i + 1), :])
 
-        def keys(m, add_engine):
+        def key_group(m):
             b, i = divmod(m, POS_TILES)
-            acc = project(m, NH * HD, NKV * HD)
-            rope(acc[:], NKV, i, out_1[b, :, P * i : P * (i + 1), :], add_engine)
+            return (m, NH * HD, NKV, out_1[b, :, P * i : P * (i + 1), :])
 
         def values(m):
             b, i = divmod(m, POS_TILES)
@@ -212,14 +206,17 @@ def tile_fastmultiheadattention_pa_kernel(
                 in_=plain[:].rearrange("p (h d) -> p h d", d=HD),
             )
 
-        for m in range(4):
-            queries(m, 0, nc.gpsimd)
-        for m in range(4):
-            queries(m, 1, nc.gpsimd)
-            keys(m, nc.vector)
-        for m in range(4, 8):
-            queries(m, 0, nc.gpsimd)
-            queries(m, 1, nc.gpsimd)
-            keys(m, nc.vector)
+        rope_pair([query_group(0, 0), query_group(1, 0)], nc.gpsimd)
+        rope_pair([query_group(2, 0), query_group(3, 0)], nc.gpsimd)
+        rope_pair([key_group(0), key_group(1)], nc.gpsimd)
+        rope_pair([query_group(0, 1), query_group(1, 1)], nc.gpsimd)
+        rope_pair([query_group(2, 1), query_group(3, 1)], nc.gpsimd)
+        rope_pair([key_group(2), key_group(3)], nc.gpsimd)
+        rope_pair([query_group(4, 0), query_group(4, 1)], nc.gpsimd)
+        rope_pair([query_group(5, 0), query_group(5, 1)], nc.gpsimd)
+        rope_pair([key_group(4), key_group(5)], nc.gpsimd)
+        rope_pair([query_group(6, 0), query_group(6, 1)], nc.vector)
+        rope_pair([query_group(7, 0), query_group(7, 1)], nc.vector)
+        rope_pair([key_group(6), key_group(7)], nc.vector)
         for m in range(8):
             values(m)

@@ -21,7 +21,8 @@ ALU = mybir.AluOpType
 ACT = mybir.ActivationFunctionType
 
 TWO_PI = 6.283185307179586
-WARM_UP = 8
+WARM_UP = 9
+Q0, Q1, KEYS, VALUES = 0, N_TILE, NH * HD, (NH + NKV) * HD
 
 
 def split_turns(d):
@@ -42,26 +43,24 @@ def tile_fastmultiheadattention_pa_kernel(
         work = ctx.enter_context(tc.tile_pool(name="work", bufs=4))
         psum = ctx.enter_context(tc.psum_pool(name="psum", bufs=8))
 
-        def load_codes(words, c, name, queue, view):
-            codes = keep.tile([P, PASSES, 2 * N_TILE], U8, name=name, align_bytes=64)
-            queue.dma_start(
-                out=codes[:].bitcast(view),
-                in_=words[:, :, 2 * N_TILE * c : 2 * N_TILE * (c + 1)].rearrange("g p n -> p g n").bitcast(view),
+        def load_codes(words, c0, width, name):
+            codes = keep.tile([P, PASSES, 2 * width], U8, name=name, align_bytes=64)
+            nc.sync.dma_start(
+                out=codes[:].bitcast(I32),
+                in_=words[:, :, 2 * c0 : 2 * (c0 + width)].rearrange("g p n -> p g n").bitcast(I32),
             )
             return codes
 
-        def zero_planes(name):
-            planes = keep.tile([P, PASSES, N_TILE], U8, name=name, align_bytes=64)
+        def zero_planes(width, name):
+            planes = keep.tile([P, PASSES, width], U8, name=name, align_bytes=64)
             nc.vector.memset(planes[:].bitcast(I32), 0)
             return planes
 
-        def load_planes(planes, scales, c):
+        def load_planes(planes, scales, c0, width):
             for q in range(4):
                 nc.sync.dma_start(
                     out=planes[32 * q : 32 * q + 4, :, :].bitcast(I32),
-                    in_=scales[:, 4 * q : 4 * q + 4, N_TILE * c : N_TILE * (c + 1)]
-                    .rearrange("g r n -> r g n")
-                    .bitcast(I32),
+                    in_=scales[:, 4 * q : 4 * q + 4, c0 : c0 + width].rearrange("g r n -> r g n").bitcast(I32),
                 )
 
         zero = keep.tile([P, 1], F32, name="zero")
@@ -72,38 +71,41 @@ def tile_fastmultiheadattention_pa_kernel(
         nc.gpsimd.iota(
             pos[:], pattern=[[P, POS_TILES]], base=0, channel_multiplier=1, allow_small_or_imprecise_dtypes=True
         )
-
-        h_planes = {0: zero_planes("h_planes0")}
-        w_planes = {0: zero_planes("w_planes0")}
-        load_planes(h_planes[0], hidden_states_scales, 0)
-        h_codes = {0: load_codes(hidden_states_words, 0, "h_codes0", nc.sync, I32)}
-        w_codes = {0: load_codes(W_qkv_words, 0, "w_codes0", nc.sync, I32)}
-        load_planes(w_planes[0], W_qkv_scales, 0)
-
-        if WARM_UP:
-            idle_in = keep.tile([P, N_TILE], BF16, name="idle_in")
-            nc.vector.memset(idle_in[:], 0.0)
-            idle_out = psum.tile([P, N_TILE], F32, name="acc")
-            for r in range(WARM_UP):
-                nc.tensor.matmul(out=idle_out[:], lhsT=idle_in[:, :P], rhs=idle_in[:], start=True, stop=True)
-
-        for n in (2, 1):
-            w_planes[n] = zero_planes("w_planes%d" % n)
-            w_codes[n] = load_codes(W_qkv_words, n, "w_codes%d" % n, nc.sync, I32)
-            load_planes(w_planes[n], W_qkv_scales, n)
-        h_planes[1] = zero_planes("h_planes1")
-        h_codes[1] = load_codes(hidden_states_words, 1, "h_codes1", nc.sync, I32)
-        load_planes(h_planes[1], hidden_states_scales, 1)
-
         step = keep.tile([P, 2], F32, name="step")
         nc.gpsimd.iota(step[:], pattern=[[1, 2]], base=0, channel_multiplier=0, allow_small_or_imprecise_dtypes=True)
+
+        w_widths = {Q0: N_TILE, Q1: N_TILE, KEYS: NKV * HD, VALUES: NKV * HD}
+        h_planes, h_codes, w_planes, w_codes = {}, {}, {}, {}
+        first_w = KEYS
+        h_planes[0] = zero_planes(SEQ, "h_planes0")
+        w_planes[first_w] = zero_planes(w_widths[first_w], "w_planes%d" % first_w)
+        load_planes(h_planes[0], hidden_states_scales, 0, SEQ)
+        h_codes[0] = load_codes(hidden_states_words, 0, SEQ, "h_codes0")
+        w_codes[first_w] = load_codes(W_qkv_words, first_w, w_widths[first_w], "w_codes%d" % first_w)
+        load_planes(w_planes[first_w], W_qkv_scales, first_w, w_widths[first_w])
+
+        idle_in = keep.tile([P, N_TILE], BF16, name="idle_in")
+        nc.vector.memset(idle_in[:], 0.0)
+        idle_out = psum.tile([P, N_TILE], F32, name="acc")
+        for r in range(WARM_UP):
+            nc.tensor.matmul(out=idle_out[:], lhsT=idle_in[:, :P], rhs=idle_in[:], start=True, stop=True)
+
+        for c0 in (Q0, Q1, VALUES):
+            if c0 == VALUES:
+                h_planes[1] = zero_planes(SEQ, "h_planes1")
+                h_codes[1] = load_codes(hidden_states_words, SEQ, SEQ, "h_codes1")
+                load_planes(h_planes[1], hidden_states_scales, SEQ, SEQ)
+            w_planes[c0] = zero_planes(w_widths[c0], "w_planes%d" % c0)
+            w_codes[c0] = load_codes(W_qkv_words, c0, w_widths[c0], "w_codes%d" % c0)
+            load_planes(w_planes[c0], W_qkv_scales, c0, w_widths[c0])
+
         per_turn = keep.tile([P, 2, HALF], F32, name="per_turn")
         turns_hi = keep.tile([P, POS_TILES, HALF], F32, name="turns_hi")
         turns_lo = keep.tile([P, POS_TILES, HALF], F32, name="turns_lo")
-        for part, dst, v_from in ((0, turns_hi, 40), (1, turns_lo, 40)):
+        for part, dst in ((0, turns_hi), (1, turns_lo)):
             for d in range(0, HALF, 2):
                 first, second = split_turns(d)[part], split_turns(d + 1)[part]
-                if d < v_from:
+                if d < 40:
                     nc.scalar.activation(
                         out=per_turn[:, part, d : d + 2], in_=step[:], func=ACT.Copy, scale=second - first, bias=first
                     )
@@ -116,57 +118,86 @@ def tile_fastmultiheadattention_pa_kernel(
                         op0=ALU.mult,
                         op1=ALU.add,
                     )
-            nc.vector.tensor_tensor(
-                out=dst[:],
-                in0=per_turn[:, part : part + 1, :].to_broadcast([P, POS_TILES, HALF]),
-                in1=pos[:].unsqueeze(2).to_broadcast([P, POS_TILES, HALF]),
-                op=ALU.mult,
-            )
         whole_i = keep.tile([P, POS_TILES, HALF], I32, name="whole_i")
-        nc.vector.tensor_copy(out=whole_i[:], in_=turns_hi[:])
         frac = keep.tile([P, POS_TILES, HALF], F32, name="frac")
-        nc.vector.tensor_tensor(out=frac[:], in0=turns_hi[:], in1=whole_i[:], op=ALU.subtract)
         turn = keep.tile([P, POS_TILES, HALF], F32, name="turn")
-        nc.vector.tensor_tensor(out=turn[:], in0=frac[:], in1=turns_lo[:], op=ALU.add)
         minus_c = keep.tile([P, POS_TILES, HALF], F32, name="minus_c")
-        nc.vector.scalar_tensor_tensor(
-            out=minus_c[:], in0=turn[:], scalar=0.25, in1=turn[:], op0=ALU.is_gt, op1=ALU.subtract
-        )
         minus_s = keep.tile([P, POS_TILES, HALF], F32, name="minus_s")
-        nc.vector.scalar_tensor_tensor(
-            out=minus_s[:], in0=turn[:], scalar=0.5, in1=turn[:], op0=ALU.is_gt, op1=ALU.subtract
-        )
         cos = keep.tile([P, POS_TILES, HALF], F32, name="cos")
         cross = keep.tile([P, POS_TILES, 2, HALF], F32, name="cross")
-        nc.scalar.activation(out=cos[:], in_=minus_c[:], func=ACT.Sin, scale=-TWO_PI, bias=TWO_PI / 4.0)
-        nc.scalar.activation(out=cross[:, :, 0, :], in_=minus_s[:], func=ACT.Sin, scale=TWO_PI)
-        nc.scalar.activation(out=cross[:, :, 1, :], in_=minus_s[:], func=ACT.Sin, scale=-TWO_PI)
+        sides = (slice(0, 2), slice(2, 4))
 
-        def project(m, c0, width):
+        def times_position(dst, part, side):
+            nc.vector.tensor_tensor(
+                out=dst[:, side, :],
+                in0=per_turn[:, part : part + 1, :].to_broadcast([P, 2, HALF]),
+                in1=pos[:, side].unsqueeze(2).to_broadcast([P, 2, HALF]),
+                op=ALU.mult,
+            )
+
+        for side in sides:
+            times_position(turns_hi, 0, side)
+        for side in sides:
+            nc.vector.tensor_copy(out=whole_i[:, side, :], in_=turns_hi[:, side, :])
+        for side in sides:
+            nc.vector.tensor_tensor(
+                out=frac[:, side, :], in0=turns_hi[:, side, :], in1=whole_i[:, side, :], op=ALU.subtract
+            )
+        for side in sides:
+            times_position(turns_lo, 1, side)
+        for side in sides:
+            nc.vector.tensor_tensor(out=turn[:, side, :], in0=frac[:, side, :], in1=turns_lo[:, side, :], op=ALU.add)
+        for side in sides:
+            nc.vector.scalar_tensor_tensor(
+                out=minus_c[:, side, :], in0=turn[:, side, :], scalar=0.25, in1=turn[:, side, :],
+                op0=ALU.is_gt, op1=ALU.subtract,
+            )
+        for side in sides:
+            nc.vector.scalar_tensor_tensor(
+                out=minus_s[:, side, :], in0=turn[:, side, :], scalar=0.5, in1=turn[:, side, :],
+                op0=ALU.is_gt, op1=ALU.subtract,
+            )
+        for side in sides:
+            nc.scalar.activation(
+                out=cos[:, side, :], in_=minus_c[:, side, :], func=ACT.Sin, scale=-TWO_PI, bias=TWO_PI / 4.0
+            )
+            nc.scalar.activation(out=cross[:, side, 0, :], in_=minus_s[:, side, :], func=ACT.Sin, scale=TWO_PI)
+            nc.scalar.activation(out=cross[:, side, 1, :], in_=minus_s[:, side, :], func=ACT.Sin, scale=-TWO_PI)
+
+        def project(m, c0):
             b, i = divmod(m, POS_TILES)
-            n, c = divmod(c0, N_TILE)
-            acc = psum.tile([P, width], F32, name="acc")
+            acc = psum.tile([P, w_widths[c0]], F32, name="acc")
             for g in range(PASSES):
                 nc.tensor.matmul_mx(
                     out=acc[:],
                     lhsT=h_codes[b][:, g, 2 * P * i : 2 * P * (i + 1)].bitcast(FP4X4),
                     lhsT_scale=h_planes[b][:, g, P * i : P * (i + 1)],
-                    rhs=w_codes[n][:, g, 2 * c : 2 * (c + width)].bitcast(FP4X4),
-                    rhs_scale=w_planes[n][:, g, c : c + width],
+                    rhs=w_codes[c0][:, g, :].bitcast(FP4X4),
+                    rhs_scale=w_planes[c0][:, g, :],
                     start=(g == 0),
                     stop=(g == PASSES - 1),
                 )
             return acc
 
+        def destination(m, c0):
+            b, i = divmod(m, POS_TILES)
+            rows = slice(P * i, P * (i + 1))
+            if c0 == KEYS:
+                return out_1[b, :, rows, :]
+            if c0 == VALUES:
+                return out_2[b, :, rows, :]
+            return out_0[b, c0 // HD : (c0 + N_TILE) // HD, rows, :]
+
         def rope_pair(groups, add_engine):
-            width = groups[0][2] * HD
+            width = w_widths[groups[0][1]]
+            heads = width // HD
             straight = work.tile([P, 2 * N_TILE], F32, name="straight")
             crossed = work.tile([P, 2 * N_TILE], F32, name="crossed")
             rotated = work.tile([P, 2 * N_TILE], F32, name="rotated")
-            for j, (m, c0, heads, dst) in enumerate(groups):
+            for j, (m, c0) in enumerate(groups):
                 i = m % POS_TILES
                 cols = slice(j * width, (j + 1) * width)
-                acc = project(m, c0, width)
+                acc = project(m, c0)
                 nc.vector.tensor_tensor(
                     out=straight[:, cols].rearrange("p (a d) -> p a d", d=HALF),
                     in0=acc[:].rearrange("p (a d) -> p a d", d=HALF),
@@ -182,41 +213,39 @@ def tile_fastmultiheadattention_pa_kernel(
             add_engine.tensor_tensor(
                 out=rotated[:, : 2 * width], in0=straight[:, : 2 * width], in1=crossed[:, : 2 * width], op=ALU.add
             )
-            for j, (m, c0, heads, dst) in enumerate(groups):
+            if groups[0][0] == groups[1][0]:
+                b, i = divmod(groups[0][0], POS_TILES)
                 nc.sync.dma_start(
-                    out=dst.rearrange("h p d -> p h d"),
-                    in_=rotated[:, j * width : (j + 1) * width].rearrange("p (h d) -> p h d", d=HD),
+                    out=out_0[b, :, P * i : P * (i + 1), :].rearrange("h p d -> p h d"),
+                    in_=rotated[:].rearrange("p (h d) -> p h d", d=HD),
                 )
-
-        def query_group(m, n):
-            b, i = divmod(m, POS_TILES)
-            return (m, N_TILE * n, 4, out_0[b, 4 * n : 4 * n + 4, P * i : P * (i + 1), :])
-
-        def key_group(m):
-            b, i = divmod(m, POS_TILES)
-            return (m, NH * HD, NKV, out_1[b, :, P * i : P * (i + 1), :])
+            else:
+                for j, (m, c0) in enumerate(groups):
+                    nc.sync.dma_start(
+                        out=destination(m, c0).rearrange("h p d -> p h d"),
+                        in_=rotated[:, j * width : (j + 1) * width].rearrange("p (h d) -> p h d", d=HD),
+                    )
 
         def values(m):
-            b, i = divmod(m, POS_TILES)
-            acc = project(m, (NH + NKV) * HD, NKV * HD)
+            acc = project(m, VALUES)
             plain = keep.tile([P, NKV * HD], F32, name="plain%d" % m)
             nc.scalar.copy(out=plain[:], in_=acc[:])
             nc.scalar.dma_start(
-                out=out_2[b, :, P * i : P * (i + 1), :].rearrange("h p d -> p h d"),
+                out=destination(m, VALUES).rearrange("h p d -> p h d"),
                 in_=plain[:].rearrange("p (h d) -> p h d", d=HD),
             )
 
-        rope_pair([query_group(0, 0), query_group(1, 0)], nc.gpsimd)
-        rope_pair([query_group(2, 0), query_group(3, 0)], nc.gpsimd)
-        rope_pair([key_group(0), key_group(1)], nc.gpsimd)
-        rope_pair([query_group(0, 1), query_group(1, 1)], nc.gpsimd)
-        rope_pair([query_group(2, 1), query_group(3, 1)], nc.gpsimd)
-        rope_pair([key_group(2), key_group(3)], nc.gpsimd)
-        rope_pair([query_group(4, 0), query_group(4, 1)], nc.gpsimd)
-        rope_pair([query_group(5, 0), query_group(5, 1)], nc.gpsimd)
-        rope_pair([key_group(4), key_group(5)], nc.gpsimd)
-        rope_pair([query_group(6, 0), query_group(6, 1)], nc.vector)
-        rope_pair([query_group(7, 0), query_group(7, 1)], nc.vector)
-        rope_pair([key_group(6), key_group(7)], nc.vector)
+        rope_pair([(0, KEYS), (1, KEYS)], nc.gpsimd)
+        rope_pair([(2, KEYS), (3, KEYS)], nc.gpsimd)
+        rope_pair([(0, Q0), (1, Q0)], nc.gpsimd)
+        rope_pair([(2, Q0), (3, Q0)], nc.gpsimd)
+        rope_pair([(0, Q1), (1, Q1)], nc.gpsimd)
+        rope_pair([(2, Q1), (3, Q1)], nc.gpsimd)
+        rope_pair([(4, Q0), (4, Q1)], nc.gpsimd)
+        rope_pair([(5, Q0), (5, Q1)], nc.gpsimd)
+        rope_pair([(4, KEYS), (5, KEYS)], nc.gpsimd)
+        rope_pair([(6, Q0), (6, Q1)], nc.gpsimd)
+        rope_pair([(7, Q0), (7, Q1)], nc.vector)
+        rope_pair([(6, KEYS), (7, KEYS)], nc.vector)
         for m in range(8):
             values(m)

@@ -188,9 +188,10 @@ def tile_fastmultiheadattention_pa_kernel(
                 return out_2[b, :, rows, :]
             return out_0[b, c0 // HD : (c0 + N_TILE) // HD, rows, :]
 
-        def rope_pair(groups, add_engine):
+        def rope(groups, add_engine):
             width = w_widths[groups[0][1]]
             heads = width // HD
+            used = len(groups) * width
             straight = work.tile([P, 2 * N_TILE], F32, name="straight")
             crossed = work.tile([P, 2 * N_TILE], F32, name="crossed")
             rotated = work.tile([P, 2 * N_TILE], F32, name="rotated")
@@ -211,9 +212,9 @@ def tile_fastmultiheadattention_pa_kernel(
                     op=ALU.mult,
                 )
             add_engine.tensor_tensor(
-                out=rotated[:, : 2 * width], in0=straight[:, : 2 * width], in1=crossed[:, : 2 * width], op=ALU.add
+                out=rotated[:, :used], in0=straight[:, :used], in1=crossed[:, :used], op=ALU.add
             )
-            if groups[0][0] == groups[1][0]:
+            if len(groups) == 2 and groups[0][0] == groups[1][0]:
                 b, i = divmod(groups[0][0], POS_TILES)
                 nc.sync.dma_start(
                     out=out_0[b, :, P * i : P * (i + 1), :].rearrange("h p d -> p h d"),
@@ -235,17 +236,25 @@ def tile_fastmultiheadattention_pa_kernel(
                 in_=plain[:].rearrange("p (h d) -> p h d", d=HD),
             )
 
-        rope_pair([(0, KEYS), (1, KEYS)], nc.gpsimd)
-        rope_pair([(2, KEYS), (3, KEYS)], nc.gpsimd)
-        rope_pair([(0, Q0), (1, Q0)], nc.gpsimd)
-        rope_pair([(2, Q0), (3, Q0)], nc.gpsimd)
-        rope_pair([(0, Q1), (1, Q1)], nc.gpsimd)
-        rope_pair([(2, Q1), (3, Q1)], nc.gpsimd)
-        rope_pair([(4, Q0), (4, Q1)], nc.gpsimd)
-        rope_pair([(5, Q0), (5, Q1)], nc.gpsimd)
-        rope_pair([(4, KEYS), (5, KEYS)], nc.gpsimd)
-        rope_pair([(6, Q0), (6, Q1)], nc.gpsimd)
-        rope_pair([(7, Q0), (7, Q1)], nc.vector)
-        rope_pair([(6, KEYS), (7, KEYS)], nc.vector)
-        for m in range(8):
-            values(m)
+        rope([(0, KEYS), (1, KEYS)], nc.gpsimd)
+        rope([(2, KEYS), (3, KEYS)], nc.gpsimd)
+        rope([(0, Q0), (1, Q0)], nc.gpsimd)
+        rope([(2, Q0), (3, Q0)], nc.gpsimd)
+        rope([(0, Q1), (1, Q1)], nc.gpsimd)
+        rope([(2, Q1), (3, Q1)], nc.gpsimd)
+        rope([(4, Q0), (4, Q1)], nc.gpsimd)
+        values(0)
+        rope([(5, Q0), (5, Q1)], nc.gpsimd)
+        values(1)
+        rope([(6, Q0)], nc.gpsimd)
+        rope([(6, Q1)], nc.gpsimd)
+        values(2)
+        rope([(7, Q0)], nc.gpsimd)
+        rope([(7, Q1)], nc.gpsimd)
+        values(3)
+        rope([(4, KEYS), (5, KEYS)], nc.vector)
+        values(4)
+        values(5)
+        rope([(6, KEYS), (7, KEYS)], nc.vector)
+        values(6)
+        values(7)

@@ -194,7 +194,7 @@ def tile_fastmultiheadattention_pa_kernel(
             used = len(groups) * width
             straight = work.tile([P, 2 * N_TILE], F32, name="straight")
             crossed = work.tile([P, 2 * N_TILE], F32, name="crossed")
-            rotated = work.tile([P, 2 * N_TILE], F32, name="rotated")
+            rotated = work.tile([P, 2 * N_TILE], F32, name="rotated", align_bytes=256)
             for j, (m, c0) in enumerate(groups):
                 i = m % POS_TILES
                 cols = slice(j * width, (j + 1) * width)
@@ -229,7 +229,7 @@ def tile_fastmultiheadattention_pa_kernel(
 
         def values(m):
             acc = project(m, VALUES)
-            plain = keep.tile([P, NKV * HD], F32, name="plain%d" % m)
+            plain = keep.tile([P, NKV * HD], F32, name="plain%d" % m, align_bytes=256)
             nc.scalar.copy(out=plain[:], in_=acc[:])
             nc.scalar.dma_start(
                 out=destination(m, VALUES).rearrange("h p d -> p h d"),

@@ -236,6 +236,47 @@ def tile_fastmultiheadattention_pa_kernel(
                 in_=plain[:].rearrange("p (h d) -> p h d", d=HD),
             )
 
+        def by_head_and_tile(dram, b, i):
+            return dram[b].rearrange("h (i p) d -> p (h i) d", p=P)[:, i :: 2, :]
+
+        def rope_keys(m, add_engine):
+            b, i = divmod(m, POS_TILES)
+            used = 2 * NKV * HD
+            straight = work.tile([P, 2 * N_TILE], F32, name="straight")
+            crossed = work.tile([P, 2 * N_TILE], F32, name="crossed")
+            rotated = work.tile([P, 2 * N_TILE], F32, name="rotated", align_bytes=256)
+            for j in range(2):
+                acc = project(m + 2 * j, KEYS)
+                nc.vector.tensor_tensor(
+                    out=straight[:, :used].rearrange("p (h j t d) -> p h j t d", j=2, t=2, d=HALF)[:, :, j, :, :],
+                    in0=acc[:].rearrange("p (h t d) -> p h t d", t=2, d=HALF),
+                    in1=cos[:, i + 2 * j : i + 2 * j + 1, :].unsqueeze(2).to_broadcast([P, NKV, 2, HALF]),
+                    op=ALU.mult,
+                )
+                nc.vector.tensor_tensor(
+                    out=crossed[:, :used].rearrange("p (h j t d) -> p h j t d", j=2, t=2, d=HALF)[:, :, j, :, :],
+                    in0=acc[:].rearrange("p (h t d) -> p h t d", t=2, d=HALF)[:, :, ::-1, :],
+                    in1=cross[:, i + 2 * j : i + 2 * j + 1, :, :].to_broadcast([P, NKV, 2, HALF]),
+                    op=ALU.mult,
+                )
+            add_engine.tensor_tensor(
+                out=rotated[:, :used], in0=straight[:, :used], in1=crossed[:, :used], op=ALU.add
+            )
+            nc.sync.dma_start(
+                out=by_head_and_tile(out_1, b, i), in_=rotated[:, :used].rearrange("p (x d) -> p x d", d=HD)
+            )
+
+        def values_pair(m):
+            b, i = divmod(m, POS_TILES)
+            plain = keep.tile([P, 2 * NKV * HD], F32, name="plain%d" % m, align_bytes=256)
+            for j in range(2):
+                acc = project(m + 2 * j, VALUES)
+                nc.scalar.copy(
+                    out=plain[:].rearrange("p (h j d) -> p h j d", j=2, d=HD)[:, :, j, :],
+                    in_=acc[:].rearrange("p (h d) -> p h d", d=HD),
+                )
+            nc.scalar.dma_start(out=by_head_and_tile(out_2, b, i), in_=plain[:].rearrange("p (x d) -> p x d", d=HD))
+
         rope([(0, KEYS), (1, KEYS)], nc.gpsimd)
         rope([(2, KEYS), (3, KEYS)], nc.gpsimd)
         rope([(0, Q0), (1, Q0)], nc.gpsimd)
@@ -252,9 +293,8 @@ def tile_fastmultiheadattention_pa_kernel(
         rope([(7, Q0)], nc.gpsimd)
         rope([(7, Q1)], nc.gpsimd)
         values(3)
-        rope([(4, KEYS), (5, KEYS)], nc.vector)
-        values(4)
+        rope_keys(4, nc.vector)
+        values_pair(4)
+        rope_keys(5, nc.vector)
         values(5)
-        rope([(6, KEYS), (7, KEYS)], nc.vector)
-        values(6)
         values(7)

@@ -164,16 +164,17 @@ def tile_fastmultiheadattention_pa_kernel(
             nc.scalar.activation(out=cross[:, side, 0, :], in_=minus_s[:, side, :], func=ACT.Sin, scale=TWO_PI)
             nc.scalar.activation(out=cross[:, side, 1, :], in_=minus_s[:, side, :], func=ACT.Sin, scale=-TWO_PI)
 
-        def project(m, c0):
+        def project(m, c0, first=0, width=None):
             b, i = divmod(m, POS_TILES)
-            acc = psum.tile([P, w_widths[c0]], F32, name="acc")
+            width = width or w_widths[c0]
+            acc = psum.tile([P, width], F32, name="acc")
             for g in range(PASSES):
                 nc.tensor.matmul_mx(
                     out=acc[:],
                     lhsT=h_codes[b][:, g, 2 * P * i : 2 * P * (i + 1)].bitcast(FP4X4),
                     lhsT_scale=h_planes[b][:, g, P * i : P * (i + 1)],
-                    rhs=w_codes[c0][:, g, :].bitcast(FP4X4),
-                    rhs_scale=w_planes[c0][:, g, :],
+                    rhs=w_codes[c0][:, g, 2 * first : 2 * (first + width)].bitcast(FP4X4),
+                    rhs_scale=w_planes[c0][:, g, first : first + width],
                     start=(g == 0),
                     stop=(g == PASSES - 1),
                 )
@@ -277,6 +278,14 @@ def tile_fastmultiheadattention_pa_kernel(
                 )
             nc.scalar.dma_start(out=by_head_and_tile(out_2, b, i), in_=plain[:].rearrange("p (x d) -> p x d", d=HD))
 
+        def values_by_head(m):
+            b, i = divmod(m, POS_TILES)
+            for h in range(NKV):
+                acc = project(m, VALUES, h * HD, HD)
+                plain = keep.tile([P, HD], F32, name="plain%d_%d" % (m, h), align_bytes=256)
+                nc.scalar.copy(out=plain[:], in_=acc[:])
+                nc.scalar.dma_start(out=out_2[b, h, P * i : P * (i + 1), :], in_=plain[:])
+
         rope([(0, KEYS), (1, KEYS)], nc.gpsimd)
         rope([(2, KEYS), (3, KEYS)], nc.gpsimd)
         rope([(0, Q0), (1, Q0)], nc.gpsimd)
@@ -297,4 +306,4 @@ def tile_fastmultiheadattention_pa_kernel(
         values_pair(4)
         rope_keys(5, nc.vector)
         values(5)
-        values(7)
+        values_by_head(7)

@@ -22,6 +22,7 @@ ACT = mybir.ActivationFunctionType
 
 TWO_PI = 6.283185307179586
 WARM_UP = 9
+CODES_AT, PLANES_AT = 0, 0
 Q0, Q1, KEYS, VALUES = 0, N_TILE, NH * HD, (NH + NKV) * HD
 
 
@@ -39,12 +40,21 @@ def tile_fastmultiheadattention_pa_kernel(
 ):
     nc = tc.nc
     with ExitStack() as ctx:
+        mx = ctx.enter_context(tc.tile_pool(name="mx", bufs=1))
         keep = ctx.enter_context(tc.tile_pool(name="keep", bufs=1))
         work = ctx.enter_context(tc.tile_pool(name="work", bufs=4))
         psum = ctx.enter_context(tc.psum_pool(name="psum", bufs=8))
 
+        idle_in = mx.tile([P, N_TILE], BF16, name="idle_in", align_bytes=256, offset=0)
+        cursor = [2 * N_TILE]
+
+        def place(size, at):
+            start = cursor[0] + (at - cursor[0]) % 256
+            cursor[0] = start + size
+            return start
+
         def load_codes(words, c0, width, name):
-            codes = keep.tile([P, PASSES, 2 * width], U8, name=name, align_bytes=64)
+            codes = mx.tile([P, PASSES, 2 * width], U8, name=name, offset=place(PASSES * 2 * width, CODES_AT))
             nc.sync.dma_start(
                 out=codes[:].bitcast(I32),
                 in_=words[:, :, 2 * c0 : 2 * (c0 + width)].rearrange("g p n -> p g n").bitcast(I32),
@@ -52,7 +62,7 @@ def tile_fastmultiheadattention_pa_kernel(
             return codes
 
         def zero_planes(width, name):
-            planes = keep.tile([P, PASSES, width], U8, name=name, align_bytes=64)
+            planes = mx.tile([P, PASSES, width], U8, name=name, offset=place(PASSES * width, PLANES_AT))
             nc.vector.memset(planes[:].bitcast(I32), 0)
             return planes
 
@@ -84,7 +94,6 @@ def tile_fastmultiheadattention_pa_kernel(
         w_codes[first_w] = load_codes(W_qkv_words, first_w, w_widths[first_w], "w_codes%d" % first_w)
         load_planes(w_planes[first_w], W_qkv_scales, first_w, w_widths[first_w])
 
-        idle_in = keep.tile([P, N_TILE], BF16, name="idle_in")
         nc.vector.memset(idle_in[:], 0.0)
         idle_out = psum.tile([P, N_TILE], F32, name="acc")
         for r in range(WARM_UP):

from contextlib import ExitStack

import concourse.mybir as mybir

BATCH, SEQ, HID = 2, 512, 2048
NH, NKV, HD = 8, 2, 128
HALF = HD // 2
P = 128
K_PASS = 512
PASSES = HID // K_PASS
N_TILE = 512
POS_TILES = SEQ // P
FLOPS = 2 * BATCH * SEQ * HID * (NH + 2 * NKV) * HD

F32 = mybir.dt.float32
BF16 = mybir.dt.bfloat16
I32 = mybir.dt.int32
U8 = mybir.dt.uint8
FP4X4 = mybir.dt.float4_e2m1fn_x4
ALU = mybir.AluOpType
ACT = mybir.ActivationFunctionType

TWO_PI = 6.283185307179586
WARM_UP = 9
CODES_AT, PLANES_AT = 0, 0
Q0, Q1, KEYS, VALUES = 0, N_TILE, NH * HD, (NH + NKV) * HD


def split_turns(d):
    g = 10000.0 ** (-d / 64.0) / TWO_PI
    k = 0
    while g * 2.0 ** k < 16384.0:
        k += 1
    hi = int(g * 2.0 ** k) / 2.0 ** k
    return hi, g - hi


def tile_fastmultiheadattention_pa_kernel(
    tc, hidden_states_words, hidden_states_scales, W_qkv_words, W_qkv_scales, out_0, out_1, out_2
):
    nc = tc.nc
    with ExitStack() as ctx:
        mx = ctx.enter_context(tc.tile_pool(name="mx", bufs=1))
        keep = ctx.enter_context(tc.tile_pool(name="keep", bufs=1))
        work = ctx.enter_context(tc.tile_pool(name="work", bufs=4))
        psum = ctx.enter_context(tc.psum_pool(name="psum", bufs=8))

        idle_in = mx.tile([P, N_TILE], BF16, name="idle_in", align_bytes=256, offset=0)
        cursor = [2 * N_TILE]

        def place(size, at):
            start = cursor[0] + (at - cursor[0]) % 256
            cursor[0] = start + size
            return start

        def load_codes(words, c0, width, name):
            codes = mx.tile([P, PASSES, 2 * width], U8, name=name, offset=place(PASSES * 2 * width, CODES_AT))
            nc.sync.dma_start(
                out=codes[:].bitcast(I32),
                in_=words[:, :, 2 * c0 : 2 * (c0 + width)].rearrange("g p n -> p g n").bitcast(I32),
            )
            return codes

        def zero_planes(width, name):
            planes = mx.tile([P, PASSES, width], U8, name=name, offset=place(PASSES * width, PLANES_AT))
            nc.vector.memset(planes[:].bitcast(I32), 0)
            return planes

        def load_planes(planes, scales, c0, width):
            for q in range(4):
                nc.sync.dma_start(
                    out=planes[32 * q : 32 * q + 4, :, :].bitcast(I32),
                    in_=scales[:, 4 * q : 4 * q + 4, c0 : c0 + width].rearrange("g r n -> r g n").bitcast(I32),
                )

        zero = keep.tile([P, 1], F32, name="zero")
        nc.vector.memset(zero[:], 0.0)
        warm = keep.tile([P, 1], F32, name="warm")
        nc.scalar.activation(out=warm[:], in_=zero[:], func=ACT.Sin)
        pos = keep.tile([P, POS_TILES], F32, name="pos")
        nc.gpsimd.iota(
            pos[:], pattern=[[P, POS_TILES]], base=0, channel_multiplier=1, allow_small_or_imprecise_dtypes=True
        )
        step = keep.tile([P, 2], F32, name="step")
        nc.gpsimd.iota(step[:], pattern=[[1, 2]], base=0, channel_multiplier=0, allow_small_or_imprecise_dtypes=True)

        w_widths = {Q0: N_TILE, Q1: N_TILE, KEYS: NKV * HD, VALUES: NKV * HD}
        h_planes, h_codes, w_planes, w_codes = {}, {}, {}, {}
        first_w = KEYS
        h_planes[0] = zero_planes(SEQ, "h_planes0")
        w_planes[first_w] = zero_planes(w_widths[first_w], "w_planes%d" % first_w)
        load_planes(h_planes[0], hidden_states_scales, 0, SEQ)
        h_codes[0] = load_codes(hidden_states_words, 0, SEQ, "h_codes0")
        w_codes[first_w] = load_codes(W_qkv_words, first_w, w_widths[first_w], "w_codes%d" % first_w)
        load_planes(w_planes[first_w], W_qkv_scales, first_w, w_widths[first_w])

        nc.vector.memset(idle_in[:], 0.0)
        idle_out = psum.tile([P, N_TILE], F32, name="acc")
        for r in range(WARM_UP):
            nc.tensor.matmul(out=idle_out[:], lhsT=idle_in[:, :P], rhs=idle_in[:], start=True, stop=True)

        for c0 in (Q0, Q1, VALUES):
            if c0 == VALUES:
                h_planes[1] = zero_planes(SEQ, "h_planes1")
                h_codes[1] = load_codes(hidden_states_words, SEQ, SEQ, "h_codes1")
                load_planes(h_planes[1], hidden_states_scales, SEQ, SEQ)
            w_planes[c0] = zero_planes(w_widths[c0], "w_planes%d" % c0)
            w_codes[c0] = load_codes(W_qkv_words, c0, w_widths[c0], "w_codes%d" % c0)
            load_planes(w_planes[c0], W_qkv_scales, c0, w_widths[c0])

        per_turn = keep.tile([P, 2, HALF], F32, name="per_turn")
        turns_hi = keep.tile([P, POS_TILES, HALF], F32, name="turns_hi")
        turns_lo = keep.tile([P, POS_TILES, HALF], F32, name="turns_lo")
        for part, dst in ((0, turns_hi), (1, turns_lo)):
            for d in range(0, HALF, 2):
                first, second = split_turns(d)[part], split_turns(d + 1)[part]
                if d < 40:
                    nc.scalar.activation(
                        out=per_turn[:, part, d : d + 2], in_=step[:], func=ACT.Copy, scale=second - first, bias=first
                    )
                else:
                    nc.vector.tensor_scalar(
                        out=per_turn[:, part, d : d + 2],
                        in0=step[:],
                        scalar1=second - first,
                        scalar2=first,
                        op0=ALU.mult,
                        op1=ALU.add,
                    )
        whole_i = keep.tile([P, POS_TILES, HALF], I32, name="whole_i")
        frac = keep.tile([P, POS_TILES, HALF], F32, name="frac")
        turn = keep.tile([P, POS_TILES, HALF], F32, name="turn")
        minus_c = keep.tile([P, POS_TILES, HALF], F32, name="minus_c")
        minus_s = keep.tile([P, POS_TILES, HALF], F32, name="minus_s")
        cos = keep.tile([P, POS_TILES, HALF], F32, name="cos")
        cross = keep.tile([P, POS_TILES, 2, HALF], F32, name="cross")
        sides = (slice(0, 2), slice(2, 4))

        def times_position(dst, part, side):
            nc.vector.tensor_tensor(
                out=dst[:, side, :],
                in0=per_turn[:, part : part + 1, :].to_broadcast([P, 2, HALF]),
                in1=pos[:, side].unsqueeze(2).to_broadcast([P, 2, HALF]),
                op=ALU.mult,
            )

        for side in sides:
            times_position(turns_hi, 0, side)
        for side in sides:
            nc.vector.tensor_copy(out=whole_i[:, side, :], in_=turns_hi[:, side, :])
        for side in sides:
            nc.vector.tensor_tensor(
                out=frac[:, side, :], in0=turns_hi[:, side, :], in1=whole_i[:, side, :], op=ALU.subtract
            )
        for side in sides:
            times_position(turns_lo, 1, side)
        for side in sides:
            nc.vector.tensor_tensor(out=turn[:, side, :], in0=frac[:, side, :], in1=turns_lo[:, side, :], op=ALU.add)
        for side in sides:
            nc.vector.scalar_tensor_tensor(
                out=minus_c[:, side, :], in0=turn[:, side, :], scalar=0.25, in1=turn[:, side, :],
                op0=ALU.is_gt, op1=ALU.subtract,
            )
        for side in sides:
            nc.vector.scalar_tensor_tensor(
                out=minus_s[:, side, :], in0=turn[:, side, :], scalar=0.5, in1=turn[:, side, :],
                op0=ALU.is_gt, op1=ALU.subtract,
            )
        for side in sides:
            nc.scalar.activation(
                out=cos[:, side, :], in_=minus_c[:, side, :], func=ACT.Sin, scale=-TWO_PI, bias=TWO_PI / 4.0
            )
            nc.scalar.activation(out=cross[:, side, 0, :], in_=minus_s[:, side, :], func=ACT.Sin, scale=TWO_PI)
            nc.scalar.activation(out=cross[:, side, 1, :], in_=minus_s[:, side, :], func=ACT.Sin, scale=-TWO_PI)

        def project(m, c0, first=0, width=None):
            b, i = divmod(m, POS_TILES)
            width = width or w_widths[c0]
            acc = psum.tile([P, width], F32, name="acc")
            for g in range(PASSES):
                nc.tensor.matmul_mx(
                    out=acc[:],
                    lhsT=h_codes[b][:, g, 2 * P * i : 2 * P * (i + 1)].bitcast(FP4X4),
                    lhsT_scale=h_planes[b][:, g, P * i : P * (i + 1)],
                    rhs=w_codes[c0][:, g, 2 * first : 2 * (first + width)].bitcast(FP4X4),
                    rhs_scale=w_planes[c0][:, g, first : first + width],
                    start=(g == 0),
                    stop=(g == PASSES - 1),
                )
            return acc

        def destination(m, c0):
            b, i = divmod(m, POS_TILES)
            rows = slice(P * i, P * (i + 1))
            if c0 == KEYS:
                return out_1[b, :, rows, :]
            if c0 == VALUES:
                return out_2[b, :, rows, :]
            return out_0[b, c0 // HD : (c0 + N_TILE) // HD, rows, :]

        def rope(groups, add_engine):
            width = w_widths[groups[0][1]]
            heads = width // HD
            used = len(groups) * width
            straight = work.tile([P, 2 * N_TILE], F32, name="straight")
            crossed = work.tile([P, 2 * N_TILE], F32, name="crossed")
            rotated = work.tile([P, 2 * N_TILE], F32, name="rotated", align_bytes=256)
            for j, (m, c0) in enumerate(groups):
                i = m % POS_TILES
                cols = slice(j * width, (j + 1) * width)
                acc = project(m, c0)
                nc.vector.tensor_tensor(
                    out=straight[:, cols].rearrange("p (a d) -> p a d", d=HALF),
                    in0=acc[:].rearrange("p (a d) -> p a d", d=HALF),
                    in1=cos[:, i : i + 1, :].to_broadcast([P, 2 * heads, HALF]),
                    op=ALU.mult,
                )
                nc.vector.tensor_tensor(
                    out=crossed[:, cols].rearrange("p (h t d) -> p h t d", t=2, d=HALF),
                    in0=acc[:].rearrange("p (h t d) -> p h t d", t=2, d=HALF)[:, :, ::-1, :],
                    in1=cross[:, i : i + 1, :, :].to_broadcast([P, heads, 2, HALF]),
                    op=ALU.mult,
                )
            add_engine.tensor_tensor(
                out=rotated[:, :used], in0=straight[:, :used], in1=crossed[:, :used], op=ALU.add
            )
            if len(groups) == 2 and groups[0][0] == groups[1][0]:
                b, i = divmod(groups[0][0], POS_TILES)
                nc.sync.dma_start(
                    out=out_0[b, :, P * i : P * (i + 1), :].rearrange("h p d -> p h d"),
                    in_=rotated[:].rearrange("p (h d) -> p h d", d=HD),
                )
            else:
                for j, (m, c0) in enumerate(groups):
                    nc.sync.dma_start(
                        out=destination(m, c0).rearrange("h p d -> p h d"),
                        in_=rotated[:, j * width : (j + 1) * width].rearrange("p (h d) -> p h d", d=HD),
                    )

        def values(m):
            acc = project(m, VALUES)
            plain = keep.tile([P, NKV * HD], F32, name="plain%d" % m, align_bytes=256)
            nc.scalar.copy(out=plain[:], in_=acc[:])
            nc.scalar.dma_start(
                out=destination(m, VALUES).rearrange("h p d -> p h d"),
                in_=plain[:].rearrange("p (h d) -> p h d", d=HD),
            )

        def by_head_and_tile(dram, b, i):
            return dram[b].rearrange("h (i p) d -> p (h i) d", p=P)[:, i :: 2, :]

        def rope_keys(m, add_engine):
            b, i = divmod(m, POS_TILES)
            used = 2 * NKV * HD
            straight = work.tile([P, 2 * N_TILE], F32, name="straight")
            crossed = work.tile([P, 2 * N_TILE], F32, name="crossed")
            rotated = work.tile([P, 2 * N_TILE], F32, name="rotated", align_bytes=256)
            for j in range(2):
                acc = project(m + 2 * j, KEYS)
                nc.vector.tensor_tensor(
                    out=straight[:, :used].rearrange("p (h j t d) -> p h j t d", j=2, t=2, d=HALF)[:, :, j, :, :],
                    in0=acc[:].rearrange("p (h t d) -> p h t d", t=2, d=HALF),
                    in1=cos[:, i + 2 * j : i + 2 * j + 1, :].unsqueeze(2).to_broadcast([P, NKV, 2, HALF]),
                    op=ALU.mult,
                )
                nc.vector.tensor_tensor(
                    out=crossed[:, :used].rearrange("p (h j t d) -> p h j t d", j=2, t=2, d=HALF)[:, :, j, :, :],
                    in0=acc[:].rearrange("p (h t d) -> p h t d", t=2, d=HALF)[:, :, ::-1, :],
                    in1=cross[:, i + 2 * j : i + 2 * j + 1, :, :].to_broadcast([P, NKV, 2, HALF]),
                    op=ALU.mult,
                )
            add_engine.tensor_tensor(
                out=rotated[:, :used], in0=straight[:, :used], in1=crossed[:, :used], op=ALU.add
            )
            nc.sync.dma_start(
                out=by_head_and_tile(out_1, b, i), in_=rotated[:, :used].rearrange("p (x d) -> p x d", d=HD)
            )

        def values_pair(m):
            b, i = divmod(m, POS_TILES)
            plain = keep.tile([P, 2 * NKV * HD], F32, name="plain%d" % m, align_bytes=256)
            for j in range(2):
                acc = project(m + 2 * j, VALUES)
                nc.scalar.copy(
                    out=plain[:].rearrange("p (h j d) -> p h j d", j=2, d=HD)[:, :, j, :],
                    in_=acc[:].rearrange("p (h d) -> p h d", d=HD),
                )
            nc.scalar.dma_start(out=by_head_and_tile(out_2, b, i), in_=plain[:].rearrange("p (x d) -> p x d", d=HD))

        def values_by_head(m):
            b, i = divmod(m, POS_TILES)
            for h in range(NKV):
                acc = project(m, VALUES, h * HD, HD)
                plain = keep.tile([P, HD], F32, name="plain%d_%d" % (m, h), align_bytes=256)
                nc.scalar.copy(out=plain[:], in_=acc[:])
                nc.scalar.dma_start(out=out_2[b, h, P * i : P * (i + 1), :], in_=plain[:])

        rope([(0, KEYS), (1, KEYS)], nc.gpsimd)
        rope([(2, KEYS), (3, KEYS)], nc.gpsimd)
        rope([(0, Q0), (1, Q0)], nc.gpsimd)
        rope([(2, Q0), (3, Q0)], nc.gpsimd)
        rope([(0, Q1), (1, Q1)], nc.gpsimd)
        rope([(2, Q1), (3, Q1)], nc.gpsimd)
        rope([(4, Q0), (4, Q1)], nc.gpsimd)
        values(0)
        rope([(5, Q0), (5, Q1)], nc.gpsimd)
        values(1)
        rope([(6, Q0)], nc.gpsimd)
        rope([(6, Q1)], nc.gpsimd)
        values(2)
        rope([(7, Q0)], nc.gpsimd)
        rope([(7, Q1)], nc.gpsimd)
        values(3)
        rope_keys(4, nc.vector)
        values_pair(4)
        rope_keys(5, nc.vector)
        values(5)
        values_by_head(7)
